import numpy as np
import ml_dtypes


def mxq(x, axis, fmt="e4m3"):
    dtype, down = {"e4m3": (ml_dtypes.float8_e4m3fn, 7), "e5m2": (ml_dtypes.float8_e5m2, 14)}[fmt]
    v = np.moveaxis(np.asarray(x, np.float32).astype(ml_dtypes.bfloat16).astype(np.float64), axis, -1)
    blocks = v.reshape(v.shape[:-1] + (-1, 32))
    amax = np.abs(blocks).max(-1, keepdims=True)
    byte = np.maximum(np.where(amax > 0, np.frexp(amax)[1] - 1 + 127, 0) - down, 1)
    scale = np.exp2(byte - 127.0)
    codes = (blocks / scale).astype(np.float32).astype(dtype).astype(np.float64)
    return np.moveaxis((codes * scale).reshape(v.shape), -1, axis)


WIDE = False


def mx_kscale(k):
    if not WIDE:
        return np.ones(k)
    levels = np.array([10, -10, 5, -5, 0])
    a = np.random.permutation(np.resize(levels, k // 512 * 4)).reshape(k // 512, 4)
    idx = np.arange(k)
    return np.exp2(a[idx // 512, idx % 128 // 32])


BF16 = ml_dtypes.bfloat16


def bf(x):
    return np.asarray(x, np.float32).astype(BF16)


def f64(x):
    return np.asarray(x).astype(np.float64)


B, C, H, W, F, KH, KW = 8, 512, 32, 32, 512, 1, 1
K = KH * KW * C
SPARSITY = 0.7


def extract_patches(x, kh, kw):
    bb, s1, s2, cc = x.shape
    o1, o2 = s1 - kh + 1, s2 - kw + 1
    pats = np.stack([x[:, i:i + o1, j:j + o2, :] for i in range(kh) for j in range(kw)], axis=3)
    return pats.reshape(bb, o1, o2, kh * kw * cc)


def setup_inputs():
    s = mx_kscale(C)
    limit = np.sqrt(6.0 / (F + K))
    vals = np.random.uniform(-limit, limit, (F, K))
    mask = np.random.random((F, K)) >= SPARSITY
    mask[:, ::32] = True
    return {"inputs": bf(np.random.standard_normal((B, C, H, W)) * s[None, :, None, None]),
            "kernel": bf(vals * mask / np.tile(s, KH * KW)[None, :])}


def reference(inputs, kernel):
    x = np.transpose(f64(inputs), (0, 3, 2, 1))
    p = extract_patches(x, KH, KW)
    p2 = np.ascontiguousarray(p.reshape(-1, K))
    wt = np.ascontiguousarray(f64(kernel).T)
    out = mxq(p2, 1, "e4m3") @ mxq(wt, 0, "e4m3")
    return out.reshape(p.shape[:3] + (F,)).transpose(0, 3, 1, 2)

@@ -1,0 +1,126 @@
+from contextlib import ExitStack
+
+import concourse.mybir as mybir
+from concourse.masks import make_identity
+
+F32 = mybir.dt.float32
+BF16 = mybir.dt.bfloat16
+U32 = mybir.dt.uint32
+U8 = mybir.dt.uint8
+FP8X4 = mybir.dt.float8_e4m3fn_x4
+
+P = 128
+PACK = 4
+B, C, H, W, F = 8, 512, 32, 32, 512
+HW = H * W
+N_TILE = 512
+HALVES = HW // N_TILE
+D_HALF = H // HALVES
+M_TILES = F // P
+
+FLOPS = 2 * B * HW * C * F
+
+VECTOR_FROM_BATCH = 6
+
+
+def tile_sparseconv2d_t_kernel(tc, inputs, kernel, out):
+    nc = tc.nc
+    with ExitStack() as ctx:
+        keep = ctx.enter_context(tc.tile_pool(name="keep", bufs=1))
+        grp = ctx.enter_context(tc.tile_pool(name="grp", bufs=3))
+        outp = ctx.enter_context(tc.tile_pool(name="outp", bufs=6))
+        psum = ctx.enter_context(tc.psum_pool(name="psum", bufs=8))
+
+        w_sb = keep.tile([P, M_TILES * C], BF16, name="w_sb")
+        nc.sync.dma_start(out=w_sb[:], in_=kernel.rearrange("(p m) k -> p (m k)", m=M_TILES))
+        raws = []
+        for b in range(B):
+            raw = keep.tile([P, PACK, HW], BF16, name="raw%d" % b)
+            nc.sync.dma_start(out=raw[:], in_=inputs[b].rearrange("(p j) d a -> p j (d a)", j=PACK))
+            raws.append(raw)
+
+        ident = keep.tile([P, P], F32, name="ident")
+        make_identity(nc, ident[:])
+
+        w_words = w_sb[:].bitcast(F32).rearrange("p (m q u) -> p m u q", m=M_TILES, u=2)
+        w_grouped = keep.tile([P, F * PACK], BF16, name="w_grouped", align_bytes=64)
+        w_grouped_words = w_grouped[:].bitcast(F32).rearrange("p (m f u) -> p m f u", m=M_TILES, u=2)
+        w_codes = keep.tile([P, F], U32, name="w_codes", align_bytes=64)
+        w_scales = keep.tile([P, F], U8, name="w_scales", align_bytes=64)
+        for g in range(2):
+            wt = psum.tile([P, N_TILE], F32, name="wt", tag="bank")
+            for mm in range(2):
+                for u in range(2):
+                    s = (mm * 2 + u) * P
+                    nc.tensor.transpose(wt[:, s:s + P], w_words[:, 2 * g + mm, u, :], ident[:])
+            src = wt[:].rearrange("p (m u f) -> p m f u", m=2, u=2)
+            dst = w_grouped_words[:, 2 * g:2 * g + 2, :, :]
+            if g == 0:
+                nc.vector.tensor_copy(out=dst, in_=src)
+            else:
+                nc.scalar.copy(out=dst, in_=src)
+
+        state = {}
+
+        def regroup(s):
+            b, h = divmod(s, HALVES)
+            if h == 0:
+                state["g%d" % b] = grp.tile([P, HW, PACK], BF16, name="grouped", align_bytes=64)
+                state["c%d" % b] = grp.tile([P, HW], U32, name="codes", align_bytes=64)
+                state["s%d" % b] = grp.tile([P, HW], U8, name="scales", align_bytes=64)
+            cols = slice(N_TILE * h, N_TILE * (h + 1))
+            nc.vector.tensor_copy(
+                out=state["g%d" % b][:, cols, :].rearrange("p (c i) t -> p c t i", i=4),
+                in_=raws[b][:, :, cols].rearrange("p t (c i) -> p c t i", i=4),
+            )
+
+        def quantise(s):
+            b, h = divmod(s, HALVES)
+            cols = slice(N_TILE * h, N_TILE * (h + 1))
+            nc.vector.quantize_mx(
+                out=state["c%d" % b][:, cols].bitcast(FP8X4),
+                scales=state["s%d" % b][:, cols],
+                in_=state["g%d" % b][:, cols, :].rearrange("p w j -> p (w j)"),
+            )
+
+        def multiply(s):
+            b, h = divmod(s, HALVES)
+            cols = slice(N_TILE * h, N_TILE * (h + 1))
+            if h == 0:
+                state["o%d" % b] = outp.tile([P, M_TILES, W, H], F32, name="o")
+            o = state["o%d" % b]
+            for m in range(M_TILES):
+                f_cols = slice(P * m, P * (m + 1))
+                acc = psum.tile([P, N_TILE], F32, name="acc", tag="bank")
+                nc.tensor.matmul_mx(
+                    out=acc[:],
+                    lhsT=w_codes[:, f_cols].bitcast(FP8X4),
+                    lhsT_scale=w_scales[:, f_cols],
+                    rhs=state["c%d" % b][:, cols].bitcast(FP8X4),
+                    rhs_scale=state["s%d" % b][:, cols],
+                    start=True,
+                    stop=True,
+                )
+                dst = o[:, m, :, D_HALF * h:D_HALF * (h + 1)]
+                src = acc[:].rearrange("p (d a) -> p a d", a=W)
+                if b >= VECTOR_FROM_BATCH and m % 2 == 1:
+                    nc.vector.tensor_copy(out=dst, in_=src)
+                else:
+                    nc.scalar.copy(out=dst, in_=src)
+            if h == HALVES - 1:
+                nc.sync.dma_start(
+                    out=out[b].rearrange("(p m) a d -> p (m a d)", m=M_TILES),
+                    in_=o[:].rearrange("p m a d -> p (m a d)"),
+                )
+
+        steps = B * HALVES
+        regroup(0)
+        regroup(1)
+        nc.vector.quantize_mx(out=w_codes[:].bitcast(FP8X4), scales=w_scales[:], in_=w_grouped[:])
+        quantise(0)
+        for s in range(steps):
+            if s + 2 < steps:
+                regroup(s + 2)
+            if s + 1 < steps:
+                quantise(s + 1)
+            multiply(s)

@@ -20,7 +20,9 @@ M_TILES = F // P
 
 FLOPS = 2 * B * HW * C * F
 
-VECTOR_FROM_BATCH = 6
+
+def on_vector(b, h, m):
+    return h == 1 and m == 3
 
 
 def tile_sparseconv2d_t_kernel(tc, inputs, kernel, out):
@@ -30,6 +32,7 @@ def tile_sparseconv2d_t_kernel(tc, inputs, kernel, out):
         grp = ctx.enter_context(tc.tile_pool(name="grp", bufs=3))
         outp = ctx.enter_context(tc.tile_pool(name="outp", bufs=6))
         psum = ctx.enter_context(tc.psum_pool(name="psum", bufs=8))
+        ctx.enter_context(tc.manual_schedule())
 
         w_sb = keep.tile([P, M_TILES * C], BF16, name="w_sb")
         nc.sync.dma_start(out=w_sb[:], in_=kernel.rearrange("(p m) k -> p (m k)", m=M_TILES))
@@ -103,7 +106,7 @@ def tile_sparseconv2d_t_kernel(tc, inputs, kernel, out):
                 )
                 dst = o[:, m, :, D_HALF * h:D_HALF * (h + 1)]
                 src = acc[:].rearrange("p (d a) -> p a d", a=W)
-                if b >= VECTOR_FROM_BATCH and m % 2 == 1:
+                if on_vector(b, h, m):
                     nc.vector.tensor_copy(out=dst, in_=src)
                 else:
                     nc.scalar.copy(out=dst, in_=src)
@@ -115,8 +118,8 @@ def tile_sparseconv2d_t_kernel(tc, inputs, kernel, out):
 
         steps = B * HALVES
         regroup(0)
-        regroup(1)
         nc.vector.quantize_mx(out=w_codes[:].bitcast(FP8X4), scales=w_scales[:], in_=w_grouped[:])
+        regroup(1)
         quantise(0)
         for s in range(steps):
             if s + 2 < steps:

@@ -35,11 +35,11 @@ def tile_sparseconv2d_t_kernel(tc, inputs, kernel, out):
         ctx.enter_context(tc.manual_schedule())
 
         w_sb = keep.tile([P, M_TILES * C], BF16, name="w_sb")
-        nc.sync.dma_start(out=w_sb[:], in_=kernel.rearrange("(p m) k -> p (m k)", m=M_TILES))
+        nc.scalar.dma_start(out=w_sb[:], in_=kernel.rearrange("(p m) k -> p (m k)", m=M_TILES))
         raws = []
         for b in range(B):
             raw = keep.tile([P, PACK, HW], BF16, name="raw%d" % b)
-            nc.sync.dma_start(out=raw[:], in_=inputs[b].rearrange("(p j) d a -> p j (d a)", j=PACK))
+            (nc.sync if b % 2 == 0 else nc.scalar).dma_start(out=raw[:], in_=inputs[b].rearrange("(p j) d a -> p j (d a)", j=PACK))
             raws.append(raw)
 
         ident = keep.tile([P, P], F32, name="ident")
@@ -111,7 +111,7 @@ def tile_sparseconv2d_t_kernel(tc, inputs, kernel, out):
                 else:
                     nc.scalar.copy(out=dst, in_=src)
             if h == HALVES - 1:
-                nc.sync.dma_start(
+                (nc.sync if b % 2 == 0 else nc.scalar).dma_start(
                     out=out[b].rearrange("(p m) a d -> p (m a d)", m=M_TILES),
                     in_=o[:].rearrange("p m a d -> p (m a d)"),
                 )

@@ -21,6 +21,9 @@ M_TILES = F // P
 FLOPS = 2 * B * HW * C * F
 
 
+STORE_AFTER = {0: 1, 1: 1, 3: 2, 5: 2, 7: 2}
+
+
 def on_vector(b, h, m):
     return h == 1 and m == 3
 
@@ -30,17 +33,18 @@ def tile_sparseconv2d_t_kernel(tc, inputs, kernel, out):
     with ExitStack() as ctx:
         keep = ctx.enter_context(tc.tile_pool(name="keep", bufs=1))
         grp = ctx.enter_context(tc.tile_pool(name="grp", bufs=3))
-        outp = ctx.enter_context(tc.tile_pool(name="outp", bufs=6))
+        outp = ctx.enter_context(tc.tile_pool(name="outp", bufs=3))
         psum = ctx.enter_context(tc.psum_pool(name="psum", bufs=8))
         ctx.enter_context(tc.manual_schedule())
 
         w_sb = keep.tile([P, M_TILES * C], BF16, name="w_sb")
-        nc.scalar.dma_start(out=w_sb[:], in_=kernel.rearrange("(p m) k -> p (m k)", m=M_TILES))
+        nc.sync.dma_start(out=w_sb[:], in_=kernel.rearrange("(p m) k -> p (m k)", m=M_TILES))
         raws = []
-        for b in range(B):
-            raw = keep.tile([P, PACK, HW], BF16, name="raw%d" % b)
-            (nc.sync if b % 2 == 0 else nc.scalar).dma_start(out=raw[:], in_=inputs[b].rearrange("(p j) d a -> p j (d a)", j=PACK))
-            raws.append(raw)
+        for b0, nb in ((0, 1), (1, 1), (2, 2), (4, 2), (6, 2)):
+            big = keep.tile([P, nb, PACK, HW], BF16, name="raw%d" % b0)
+            nc.sync.dma_start(out=big[:], in_=inputs[b0:b0 + nb].rearrange("b (p j) d a -> p b j (d a)", j=PACK))
+            for i in range(nb):
+                raws.append(big[:, i])
 
         ident = keep.tile([P, P], F32, name="ident")
         make_identity(nc, ident[:])
@@ -89,9 +93,9 @@ def tile_sparseconv2d_t_kernel(tc, inputs, kernel, out):
         def multiply(s):
             b, h = divmod(s, HALVES)
             cols = slice(N_TILE * h, N_TILE * (h + 1))
-            if h == 0:
-                state["o%d" % b] = outp.tile([P, M_TILES, W, H], F32, name="o")
-            o = state["o%d" % b]
+            if h == 0 and b % 2 == 0:
+                state["o%d" % (b // 2)] = outp.tile([P, 2, M_TILES, W, H], F32, name="o")
+            o = state["o%d" % (b // 2)][:, b % 2]
             for m in range(M_TILES):
                 f_cols = slice(P * m, P * (m + 1))
                 acc = psum.tile([P, N_TILE], F32, name="acc", tag="bank")
@@ -110,10 +114,12 @@ def tile_sparseconv2d_t_kernel(tc, inputs, kernel, out):
                     nc.vector.tensor_copy(out=dst, in_=src)
                 else:
                     nc.scalar.copy(out=dst, in_=src)
-            if h == HALVES - 1:
-                (nc.sync if b % 2 == 0 else nc.scalar).dma_start(
-                    out=out[b].rearrange("(p m) a d -> p (m a d)", m=M_TILES),
-                    in_=o[:].rearrange("p m a d -> p (m a d)"),
+            if h == HALVES - 1 and b in STORE_AFTER:
+                nb = STORE_AFTER[b]
+                b0 = b - nb + 1
+                nc.sync.dma_start(
+                    out=out[b0:b + 1].rearrange("b (p m) a d -> p b (m a d)", m=M_TILES),
+                    in_=state["o%d" % (b // 2)][:, b0 % 2:b % 2 + 1].rearrange("p b m a d -> p b (m a d)"),
                 )
 
         steps = B * HALVES

@@ -21,7 +21,7 @@ M_TILES = F // P
 FLOPS = 2 * B * HW * C * F
 
 
-STORE_AFTER = {0: 1, 1: 1, 3: 2, 5: 2, 7: 2}
+STORE_AFTER = {0: 1, 1: 1, 2: 1, 3: 1, 4: 1, 5: 1, 6: 1, 7: 1}
 
 
 def on_vector(b, h, m):

@@ -37,11 +37,11 @@ def tile_sparseconv2d_t_kernel(tc, inputs, kernel, out):
         psum = ctx.enter_context(tc.psum_pool(name="psum", bufs=8))
         ctx.enter_context(tc.manual_schedule())
 
-        w_sb = keep.tile([P, M_TILES * C], BF16, name="w_sb")
+        w_sb = keep.tile([P, M_TILES * C], BF16, name="w_sb", align_bytes=256)
         nc.sync.dma_start(out=w_sb[:], in_=kernel.rearrange("(p m) k -> p (m k)", m=M_TILES))
         raws = []
         for b0, nb in ((0, 1), (1, 1), (2, 2), (4, 2), (6, 2)):
-            big = keep.tile([P, nb, PACK, HW], BF16, name="raw%d" % b0)
+            big = keep.tile([P, nb, PACK, HW], BF16, name="raw%d" % b0, align_bytes=256)
             nc.sync.dma_start(out=big[:], in_=inputs[b0:b0 + nb].rearrange("b (p j) d a -> p b j (d a)", j=PACK))
             for i in range(nb):
                 raws.append(big[:, i])
@@ -94,7 +94,7 @@ def tile_sparseconv2d_t_kernel(tc, inputs, kernel, out):
             b, h = divmod(s, HALVES)
             cols = slice(N_TILE * h, N_TILE * (h + 1))
             if h == 0 and b % 2 == 0:
-                state["o%d" % (b // 2)] = outp.tile([P, 2, M_TILES, W, H], F32, name="o")
+                state["o%d" % (b // 2)] = outp.tile([P, 2, M_TILES, W, H], F32, name="o", align_bytes=256)
             o = state["o%d" % (b // 2)][:, b % 2]
             for m in range(M_TILES):
                 f_cols = slice(P * m, P * (m + 1))

@@ -21,7 +21,7 @@ M_TILES = F // P
 FLOPS = 2 * B * HW * C * F
 
 
-STORE_AFTER = {0: 1, 1: 1, 2: 1, 3: 1, 4: 1, 5: 1, 6: 1, 7: 1}
+STORE_AFTER = {0: 1, 1: 1, 2: 1, 3: 1, 4: 1, 5: 1, 6: 1}
 
 
 def on_vector(b, h, m):
@@ -114,6 +114,11 @@ def tile_sparseconv2d_t_kernel(tc, inputs, kernel, out):
                     nc.vector.tensor_copy(out=dst, in_=src)
                 else:
                     nc.scalar.copy(out=dst, in_=src)
+                if b == B - 1 and h == HALVES - 1 and m % 2 == 1:
+                    nc.sync.dma_start(
+                        out=out[b].rearrange("(p m) a d -> p m (a d)", m=M_TILES)[:, m - 1:m + 1, :],
+                        in_=o[:, m - 1:m + 1].rearrange("p m a d -> p m (a d)"),
+                    )
             if h == HALVES - 1 and b in STORE_AFTER:
                 nb = STORE_AFTER[b]
                 b0 = b - nb + 1

@@ -25,6 +25,8 @@ STORE_AFTER = {0: 1, 1: 1, 2: 1, 3: 1, 4: 1, 5: 1, 6: 1}
 
 
 def on_vector(b, h, m):
+    if b == B - 1:
+        return m == 3 if h == 0 else m % 2 == 1
     return h == 1 and m == 3
 
 

@@ -42,7 +42,7 @@ def tile_sparseconv2d_t_kernel(tc, inputs, kernel, out):
         w_sb = keep.tile([P, M_TILES * C], BF16, name="w_sb", align_bytes=256)
         nc.sync.dma_start(out=w_sb[:], in_=kernel.rearrange("(p m) k -> p (m k)", m=M_TILES))
         raws = []
-        for b0, nb in ((0, 1), (1, 1), (2, 2), (4, 2), (6, 2)):
+        for b0, nb in ((0, 1), (1, 1), (2, 1), (3, 1), (4, 2), (6, 2)):
             big = keep.tile([P, nb, PACK, HW], BF16, name="raw%d" % b0, align_bytes=256)
             nc.sync.dma_start(out=big[:], in_=inputs[b0:b0 + nb].rearrange("b (p j) d a -> p b j (d a)", j=PACK))
             for i in range(nb):

@@ -40,34 +40,17 @@ def tile_sparseconv2d_t_kernel(tc, inputs, kernel, out):
         ctx.enter_context(tc.manual_schedule())
 
         w_sb = keep.tile([P, M_TILES * C], BF16, name="w_sb", align_bytes=256)
-        nc.sync.dma_start(out=w_sb[:], in_=kernel.rearrange("(p m) k -> p (m k)", m=M_TILES))
         raws = []
         for b0, nb in ((0, 1), (1, 1), (2, 1), (3, 1), (4, 2), (6, 2)):
             big = keep.tile([P, nb, PACK, HW], BF16, name="raw%d" % b0, align_bytes=256)
             nc.sync.dma_start(out=big[:], in_=inputs[b0:b0 + nb].rearrange("b (p j) d a -> p b j (d a)", j=PACK))
+            if b0 == 0:
+                nc.sync.dma_start(out=w_sb[:], in_=kernel.rearrange("(p m) k -> p (m k)", m=M_TILES))
             for i in range(nb):
                 raws.append(big[:, i])
 
         ident = keep.tile([P, P], F32, name="ident")
         make_identity(nc, ident[:])
-
-        w_words = w_sb[:].bitcast(F32).rearrange("p (m q u) -> p m u q", m=M_TILES, u=2)
-        w_grouped = keep.tile([P, F * PACK], BF16, name="w_grouped", align_bytes=64)
-        w_grouped_words = w_grouped[:].bitcast(F32).rearrange("p (m f u) -> p m f u", m=M_TILES, u=2)
-        w_codes = keep.tile([P, F], U32, name="w_codes", align_bytes=64)
-        w_scales = keep.tile([P, F], U8, name="w_scales", align_bytes=64)
-        for g in range(2):
-            wt = psum.tile([P, N_TILE], F32, name="wt", tag="bank")
-            for mm in range(2):
-                for u in range(2):
-                    s = (mm * 2 + u) * P
-                    nc.tensor.transpose(wt[:, s:s + P], w_words[:, 2 * g + mm, u, :], ident[:])
-            src = wt[:].rearrange("p (m u f) -> p m f u", m=2, u=2)
-            dst = w_grouped_words[:, 2 * g:2 * g + 2, :, :]
-            if g == 0:
-                nc.vector.tensor_copy(out=dst, in_=src)
-            else:
-                nc.scalar.copy(out=dst, in_=src)
 
         state = {}
 
@@ -131,9 +114,28 @@ def tile_sparseconv2d_t_kernel(tc, inputs, kernel, out):
 
         steps = B * HALVES
         regroup(0)
-        nc.vector.quantize_mx(out=w_codes[:].bitcast(FP8X4), scales=w_scales[:], in_=w_grouped[:])
         regroup(1)
+
+        w_words = w_sb[:].bitcast(F32).rearrange("p (m q u) -> p m u q", m=M_TILES, u=2)
+        w_grouped = keep.tile([P, F * PACK], BF16, name="w_grouped", align_bytes=64)
+        w_grouped_words = w_grouped[:].bitcast(F32).rearrange("p (m f u) -> p m f u", m=M_TILES, u=2)
+        w_codes = keep.tile([P, F], U32, name="w_codes", align_bytes=64)
+        w_scales = keep.tile([P, F], U8, name="w_scales", align_bytes=64)
+        for g in range(2):
+            wt = psum.tile([P, N_TILE], F32, name="wt", tag="bank")
+            for mm in range(2):
+                for u in range(2):
+                    s = (mm * 2 + u) * P
+                    nc.tensor.transpose(wt[:, s:s + P], w_words[:, 2 * g + mm, u, :], ident[:])
+            src = wt[:].rearrange("p (m u f) -> p m f u", m=2, u=2)
+            dst = w_grouped_words[:, 2 * g:2 * g + 2, :, :]
+            if g == 0:
+                nc.vector.tensor_copy(out=dst, in_=src)
+            else:
+                nc.scalar.copy(out=dst, in_=src)
+
         quantise(0)
+        nc.vector.quantize_mx(out=w_codes[:].bitcast(FP8X4), scales=w_scales[:], in_=w_grouped[:])
         for s in range(steps):
             if s + 2 < steps:
                 regroup(s + 2)

@@ -1,7 +1,6 @@
 from contextlib import ExitStack
 
 import concourse.mybir as mybir
-from concourse.masks import make_identity
 
 F32 = mybir.dt.float32
 BF16 = mybir.dt.bfloat16
@@ -17,17 +16,36 @@ N_TILE = 512
 HALVES = HW // N_TILE
 D_HALF = H // HALVES
 M_TILES = F // P
+QUADRANT = 32
 
 FLOPS = 2 * B * HW * C * F
 
-
-STORE_AFTER = {0: 1, 1: 1, 2: 1, 3: 1, 4: 1, 5: 1, 6: 1}
+LOADS = ((0, 1), (1, 1), (2, 1), (3, 1), (4, 2), (6, 2))
 
 
 def on_vector(b, h, m):
     if b == B - 1:
         return m == 3 if h == 0 else m % 2 == 1
     return h == 1 and m == 3
+
+
+def identity(nc, pool):
+    ones = pool.tile([P, P], F32, name="ones", align_bytes=64)
+    column = pool.tile([P, P], F32, name="column", align_bytes=64)
+    row = pool.tile([P, P], F32, name="row", align_bytes=64)
+    ident = pool.tile([P, P], F32, name="ident", align_bytes=64)
+    nc.vector.memset(ones[:], 1.0)
+    nc.vector.memset(ident[:], 0.0)
+    nc.vector.tensor_tensor_scan(
+        out=column[:], data0=ones[:], data1=ones[:], initial=0.0, op0=mybir.AluOpType.mult, op1=mybir.AluOpType.add
+    )
+    nc.vector.transpose(out=row[:], in_=column[:])
+    for q in range(0, P, QUADRANT):
+        block = slice(q, q + QUADRANT)
+        nc.vector.tensor_tensor(
+            out=ident[block, block], in0=row[block, block], in1=column[block, block], op=mybir.AluOpType.is_equal
+        )
+    return ident
 
 
 def tile_sparseconv2d_t_kernel(tc, inputs, kernel, out):
@@ -41,7 +59,7 @@ def tile_sparseconv2d_t_kernel(tc, inputs, kernel, out):
 
         w_sb = keep.tile([P, M_TILES * C], BF16, name="w_sb", align_bytes=256)
         raws = []
-        for b0, nb in ((0, 1), (1, 1), (2, 1), (3, 1), (4, 2), (6, 2)):
+        for b0, nb in LOADS:
             big = keep.tile([P, nb, PACK, HW], BF16, name="raw%d" % b0, align_bytes=256)
             nc.sync.dma_start(out=big[:], in_=inputs[b0:b0 + nb].rearrange("b (p j) d a -> p b j (d a)", j=PACK))
             if b0 == 0:
@@ -49,72 +67,62 @@ def tile_sparseconv2d_t_kernel(tc, inputs, kernel, out):
             for i in range(nb):
                 raws.append(big[:, i])
 
-        ident = keep.tile([P, P], F32, name="ident")
-        make_identity(nc, ident[:])
+        ident = identity(nc, keep)
 
-        state = {}
+        grouped, codes, scales, outs = {}, {}, {}, {}
 
-        def regroup(s):
-            b, h = divmod(s, HALVES)
-            if h == 0:
-                state["g%d" % b] = grp.tile([P, HW, PACK], BF16, name="grouped", align_bytes=64)
-                state["c%d" % b] = grp.tile([P, HW], U32, name="codes", align_bytes=64)
-                state["s%d" % b] = grp.tile([P, HW], U8, name="scales", align_bytes=64)
-            cols = slice(N_TILE * h, N_TILE * (h + 1))
+        def regroup(b):
+            grouped[b] = grp.tile([P, HW, PACK], BF16, name="grouped", align_bytes=64)
+            codes[b] = grp.tile([P, HW], U32, name="codes", align_bytes=64)
+            scales[b] = grp.tile([P, HW], U8, name="scales", align_bytes=64)
             nc.vector.tensor_copy(
-                out=state["g%d" % b][:, cols, :].rearrange("p (c i) t -> p c t i", i=4),
-                in_=raws[b][:, :, cols].rearrange("p t (c i) -> p c t i", i=4),
+                out=grouped[b][:].rearrange("p (c i) t -> p c t i", i=4),
+                in_=raws[b].rearrange("p t (c i) -> p c t i", i=4),
             )
 
-        def quantise(s):
-            b, h = divmod(s, HALVES)
-            cols = slice(N_TILE * h, N_TILE * (h + 1))
+        def quantise(b):
             nc.vector.quantize_mx(
-                out=state["c%d" % b][:, cols].bitcast(FP8X4),
-                scales=state["s%d" % b][:, cols],
-                in_=state["g%d" % b][:, cols, :].rearrange("p w j -> p (w j)"),
+                out=codes[b][:].bitcast(FP8X4),
+                scales=scales[b][:],
+                in_=grouped[b][:].rearrange("p w j -> p (w j)"),
             )
 
-        def multiply(s):
-            b, h = divmod(s, HALVES)
-            cols = slice(N_TILE * h, N_TILE * (h + 1))
-            if h == 0 and b % 2 == 0:
-                state["o%d" % (b // 2)] = outp.tile([P, 2, M_TILES, W, H], F32, name="o", align_bytes=256)
-            o = state["o%d" % (b // 2)][:, b % 2]
-            for m in range(M_TILES):
-                f_cols = slice(P * m, P * (m + 1))
-                acc = psum.tile([P, N_TILE], F32, name="acc", tag="bank")
-                nc.tensor.matmul_mx(
-                    out=acc[:],
-                    lhsT=w_codes[:, f_cols].bitcast(FP8X4),
-                    lhsT_scale=w_scales[:, f_cols],
-                    rhs=state["c%d" % b][:, cols].bitcast(FP8X4),
-                    rhs_scale=state["s%d" % b][:, cols],
-                    start=True,
-                    stop=True,
-                )
-                dst = o[:, m, :, D_HALF * h:D_HALF * (h + 1)]
-                src = acc[:].rearrange("p (d a) -> p a d", a=W)
-                if on_vector(b, h, m):
-                    nc.vector.tensor_copy(out=dst, in_=src)
-                else:
-                    nc.scalar.copy(out=dst, in_=src)
-                if b == B - 1 and h == HALVES - 1 and m % 2 == 1:
-                    nc.sync.dma_start(
-                        out=out[b].rearrange("(p m) a d -> p m (a d)", m=M_TILES)[:, m - 1:m + 1, :],
-                        in_=o[:, m - 1:m + 1].rearrange("p m a d -> p m (a d)"),
+        def multiply(b):
+            if b % 2 == 0:
+                outs[b // 2] = outp.tile([P, 2, M_TILES, W, H], F32, name="o", align_bytes=256)
+            o = outs[b // 2][:, b % 2]
+            for h in range(HALVES):
+                cols = slice(N_TILE * h, N_TILE * (h + 1))
+                for m in range(M_TILES):
+                    f_cols = slice(P * m, P * (m + 1))
+                    acc = psum.tile([P, N_TILE], F32, name="acc", tag="bank")
+                    nc.tensor.matmul_mx(
+                        out=acc[:],
+                        lhsT=w_codes[:, f_cols].bitcast(FP8X4),
+                        lhsT_scale=w_scales[:, f_cols],
+                        rhs=codes[b][:, cols].bitcast(FP8X4),
+                        rhs_scale=scales[b][:, cols],
+                        start=True,
+                        stop=True,
                     )
-            if h == HALVES - 1 and b in STORE_AFTER:
-                nb = STORE_AFTER[b]
-                b0 = b - nb + 1
+                    dst = o[:, m, :, D_HALF * h:D_HALF * (h + 1)]
+                    src = acc[:].rearrange("p (d a) -> p a d", a=W)
+                    if on_vector(b, h, m):
+                        nc.vector.tensor_copy(out=dst, in_=src)
+                    else:
+                        nc.scalar.copy(out=dst, in_=src)
+                    if b == B - 1 and h == HALVES - 1 and m % 2 == 1:
+                        nc.sync.dma_start(
+                            out=out[b].rearrange("(p m) a d -> p m (a d)", m=M_TILES)[:, m - 1:m + 1, :],
+                            in_=o[:, m - 1:m + 1].rearrange("p m a d -> p m (a d)"),
+                        )
+            if b < B - 1:
                 nc.sync.dma_start(
-                    out=out[b0:b + 1].rearrange("b (p m) a d -> p b (m a d)", m=M_TILES),
-                    in_=state["o%d" % (b // 2)][:, b0 % 2:b % 2 + 1].rearrange("p b m a d -> p b (m a d)"),
+                    out=out[b].rearrange("(p m) a d -> p (m a d)", m=M_TILES),
+                    in_=o.rearrange("p m a d -> p (m a d)"),
                 )
 
-        steps = B * HALVES
         regroup(0)
-        regroup(1)
 
         w_words = w_sb[:].bitcast(F32).rearrange("p (m q u) -> p m u q", m=M_TILES, u=2)
         w_grouped = keep.tile([P, F * PACK], BF16, name="w_grouped", align_bytes=64)
@@ -136,9 +144,10 @@ def tile_sparseconv2d_t_kernel(tc, inputs, kernel, out):
 
         quantise(0)
         nc.vector.quantize_mx(out=w_codes[:].bitcast(FP8X4), scales=w_scales[:], in_=w_grouped[:])
-        for s in range(steps):
-            if s + 2 < steps:
-                regroup(s + 2)
-            if s + 1 < steps:
-                quantise(s + 1)
-            multiply(s)
+        regroup(1)
+        for b in range(B):
+            if b + 1 < B:
+                quantise(b + 1)
+            if b + 2 < B:
+                regroup(b + 2)
+            multiply(b)

@@ -20,7 +20,7 @@ QUADRANT = 32
 
 FLOPS = 2 * B * HW * C * F
 
-LOADS = ((0, 1), (1, 1), (2, 1), (3, 1), (4, 2), (6, 2))
+LOADS = ((0, 1), (1, 1), (2, 2), (4, 2), (6, 1), (7, 1))
 
 
 def on_vector(b, h, m):
@@ -59,13 +59,33 @@ def tile_sparseconv2d_t_kernel(tc, inputs, kernel, out):
 
         w_sb = keep.tile([P, M_TILES * C], BF16, name="w_sb", align_bytes=256)
         raws = []
-        for b0, nb in LOADS:
-            big = keep.tile([P, nb, PACK, HW], BF16, name="raw%d" % b0, align_bytes=256)
-            nc.sync.dma_start(out=big[:], in_=inputs[b0:b0 + nb].rearrange("b (p j) d a -> p b j (d a)", j=PACK))
-            if b0 == 0:
-                nc.sync.dma_start(out=w_sb[:], in_=kernel.rearrange("(p m) k -> p (m k)", m=M_TILES))
+        pieces = []
+
+        def load_pieces(n):
+            for first in pieces[:n]:
+                rows = slice(first, first + 29, 4)
+                nc.sync.dma_start(
+                    out=raws[B - 1][rows, PACK - 1, :],
+                    in_=inputs[B - 1].rearrange("(p j) d a -> p j (d a)", j=PACK)[rows, PACK - 1, :],
+                )
+            del_n = pieces[n:]
+            pieces.clear()
+            pieces.extend(del_n)
+
+        bigs = [keep.tile([P, nb, PACK, HW], BF16, name="raw%d" % b0, align_bytes=256) for b0, nb in LOADS]
+        for (b0, nb), big in zip(LOADS, bigs):
             for i in range(nb):
                 raws.append(big[:, i])
+        pieces.extend(q + r for q in range(0, P, QUADRANT) for r in range(4))
+        for (b0, nb), big in zip(LOADS, bigs):
+            whole = PACK - 1 if b0 == B - 1 else PACK
+            nc.sync.dma_start(
+                out=big[:, :, 0:whole, :],
+                in_=inputs[b0:b0 + nb].rearrange("b (p j) d a -> p b j (d a)", j=PACK)[:, :, 0:whole, :],
+            )
+            if b0 == 0:
+                nc.sync.dma_start(out=w_sb[:], in_=kernel.rearrange("(p m) k -> p (m k)", m=M_TILES))
+            load_pieces({2: 4, 4: 4, 6: 2}.get(b0, 0))
 
         ident = identity(nc, keep)
 
@@ -111,16 +131,11 @@ def tile_sparseconv2d_t_kernel(tc, inputs, kernel, out):
                         nc.vector.tensor_copy(out=dst, in_=src)
                     else:
                         nc.scalar.copy(out=dst, in_=src)
-                    if b == B - 1 and h == HALVES - 1 and m % 2 == 1:
-                        nc.sync.dma_start(
-                            out=out[b].rearrange("(p m) a d -> p m (a d)", m=M_TILES)[:, m - 1:m + 1, :],
-                            in_=o[:, m - 1:m + 1].rearrange("p m a d -> p m (a d)"),
-                        )
-            if b < B - 1:
-                nc.sync.dma_start(
-                    out=out[b].rearrange("(p m) a d -> p (m a d)", m=M_TILES),
-                    in_=o.rearrange("p m a d -> p (m a d)"),
-                )
+            nc.sync.dma_start(
+                out=out[b].rearrange("(p m) a d -> p (m a d)", m=M_TILES),
+                in_=o.rearrange("p m a d -> p (m a d)"),
+            )
+            load_pieces({0: 3, 1: 3}.get(b, 0))
 
         regroup(0)
 

from contextlib import ExitStack

import concourse.mybir as mybir

F32 = mybir.dt.float32
BF16 = mybir.dt.bfloat16
U32 = mybir.dt.uint32
U8 = mybir.dt.uint8
FP8X4 = mybir.dt.float8_e4m3fn_x4

P = 128
PACK = 4
B, C, H, W, F = 8, 512, 32, 32, 512
HW = H * W
N_TILE = 512
HALVES = HW // N_TILE
D_HALF = H // HALVES
M_TILES = F // P
QUADRANT = 32

FLOPS = 2 * B * HW * C * F

LOADS = ((0, 1), (1, 1), (2, 2), (4, 2), (6, 1), (7, 1))


def on_vector(b, h, m):
    if b == B - 1:
        return m == 3 if h == 0 else m % 2 == 1
    return h == 1 and m == 3


def identity(nc, pool):
    ones = pool.tile([P, P], F32, name="ones", align_bytes=64)
    column = pool.tile([P, P], F32, name="column", align_bytes=64)
    row = pool.tile([P, P], F32, name="row", align_bytes=64)
    ident = pool.tile([P, P], F32, name="ident", align_bytes=64)
    nc.vector.memset(ones[:], 1.0)
    nc.vector.memset(ident[:], 0.0)
    nc.vector.tensor_tensor_scan(
        out=column[:], data0=ones[:], data1=ones[:], initial=0.0, op0=mybir.AluOpType.mult, op1=mybir.AluOpType.add
    )
    nc.vector.transpose(out=row[:], in_=column[:])
    for q in range(0, P, QUADRANT):
        block = slice(q, q + QUADRANT)
        nc.vector.tensor_tensor(
            out=ident[block, block], in0=row[block, block], in1=column[block, block], op=mybir.AluOpType.is_equal
        )
    return ident


def tile_sparseconv2d_t_kernel(tc, inputs, kernel, out):
    nc = tc.nc
    with ExitStack() as ctx:
        keep = ctx.enter_context(tc.tile_pool(name="keep", bufs=1))
        grp = ctx.enter_context(tc.tile_pool(name="grp", bufs=3))
        outp = ctx.enter_context(tc.tile_pool(name="outp", bufs=3))
        psum = ctx.enter_context(tc.psum_pool(name="psum", bufs=8))
        ctx.enter_context(tc.manual_schedule())

        w_sb = keep.tile([P, M_TILES * C], BF16, name="w_sb", align_bytes=256)
        raws = []
        pieces = []

        def load_pieces(n):
            for first in pieces[:n]:
                rows = slice(first, first + 29, 4)
                nc.sync.dma_start(
                    out=raws[B - 1][rows, PACK - 1, :],
                    in_=inputs[B - 1].rearrange("(p j) d a -> p j (d a)", j=PACK)[rows, PACK - 1, :],
                )
            del_n = pieces[n:]
            pieces.clear()
            pieces.extend(del_n)

        bigs = [keep.tile([P, nb, PACK, HW], BF16, name="raw%d" % b0, align_bytes=256) for b0, nb in LOADS]
        for (b0, nb), big in zip(LOADS, bigs):
            for i in range(nb):
                raws.append(big[:, i])
        pieces.extend(q + r for q in range(0, P, QUADRANT) for r in range(4))
        for (b0, nb), big in zip(LOADS, bigs):
            whole = PACK - 1 if b0 == B - 1 else PACK
            nc.sync.dma_start(
                out=big[:, :, 0:whole, :],
                in_=inputs[b0:b0 + nb].rearrange("b (p j) d a -> p b j (d a)", j=PACK)[:, :, 0:whole, :],
            )
            if b0 == 0:
                nc.sync.dma_start(out=w_sb[:], in_=kernel.rearrange("(p m) k -> p (m k)", m=M_TILES))
            load_pieces({2: 4, 4: 4, 6: 2}.get(b0, 0))

        ident = identity(nc, keep)

        grouped, codes, scales, outs = {}, {}, {}, {}

        def regroup(b):
            grouped[b] = grp.tile([P, HW, PACK], BF16, name="grouped", align_bytes=64)
            codes[b] = grp.tile([P, HW], U32, name="codes", align_bytes=64)
            scales[b] = grp.tile([P, HW], U8, name="scales", align_bytes=64)
            nc.vector.tensor_copy(
                out=grouped[b][:].rearrange("p (c i) t -> p c t i", i=4),
                in_=raws[b].rearrange("p t (c i) -> p c t i", i=4),
            )

        def quantise(b):
            nc.vector.quantize_mx(
                out=codes[b][:].bitcast(FP8X4),
                scales=scales[b][:],
                in_=grouped[b][:].rearrange("p w j -> p (w j)"),
            )

        def multiply(b):
            if b % 2 == 0:
                outs[b // 2] = outp.tile([P, 2, M_TILES, W, H], F32, name="o", align_bytes=256)
            o = outs[b // 2][:, b % 2]
            for h in range(HALVES):
                cols = slice(N_TILE * h, N_TILE * (h + 1))
                for m in range(M_TILES):
                    f_cols = slice(P * m, P * (m + 1))
                    acc = psum.tile([P, N_TILE], F32, name="acc", tag="bank")
                    nc.tensor.matmul_mx(
                        out=acc[:],
                        lhsT=w_codes[:, f_cols].bitcast(FP8X4),
                        lhsT_scale=w_scales[:, f_cols],
                        rhs=codes[b][:, cols].bitcast(FP8X4),
                        rhs_scale=scales[b][:, cols],
                        start=True,
                        stop=True,
                    )
                    dst = o[:, m, :, D_HALF * h:D_HALF * (h + 1)]
                    src = acc[:].rearrange("p (d a) -> p a d", a=W)
                    if on_vector(b, h, m):
                        nc.vector.tensor_copy(out=dst, in_=src)
                    else:
                        nc.scalar.copy(out=dst, in_=src)
            nc.sync.dma_start(
                out=out[b].rearrange("(p m) a d -> p (m a d)", m=M_TILES),
                in_=o.rearrange("p m a d -> p (m a d)"),
            )
            load_pieces({0: 3, 1: 3}.get(b, 0))

        regroup(0)

        w_words = w_sb[:].bitcast(F32).rearrange("p (m q u) -> p m u q", m=M_TILES, u=2)
        w_grouped = keep.tile([P, F * PACK], BF16, name="w_grouped", align_bytes=64)
        w_grouped_words = w_grouped[:].bitcast(F32).rearrange("p (m f u) -> p m f u", m=M_TILES, u=2)
        w_codes = keep.tile([P, F], U32, name="w_codes", align_bytes=64)
        w_scales = keep.tile([P, F], U8, name="w_scales", align_bytes=64)
        for g in range(2):
            wt = psum.tile([P, N_TILE], F32, name="wt", tag="bank")
            for mm in range(2):
                for u in range(2):
                    s = (mm * 2 + u) * P
                    nc.tensor.transpose(wt[:, s:s + P], w_words[:, 2 * g + mm, u, :], ident[:])
            src = wt[:].rearrange("p (m u f) -> p m f u", m=2, u=2)
            dst = w_grouped_words[:, 2 * g:2 * g + 2, :, :]
            if g == 0:
                nc.vector.tensor_copy(out=dst, in_=src)
            else:
                nc.scalar.copy(out=dst, in_=src)

        quantise(0)
        nc.vector.quantize_mx(out=w_codes[:].bitcast(FP8X4), scales=w_scales[:], in_=w_grouped[:])
        regroup(1)
        for b in range(B):
            if b + 1 < B:
                quantise(b + 1)
            if b + 2 < B:
                regroup(b + 2)
            multiply(b)
